import numpy as np
import ml_dtypes


def mxq(x, axis, fmt="e4m3"):
    dtype, down = {"e4m3": (ml_dtypes.float8_e4m3fn, 7), "e5m2": (ml_dtypes.float8_e5m2, 14)}[fmt]
    v = np.moveaxis(np.asarray(x, np.float32).astype(ml_dtypes.bfloat16).astype(np.float64), axis, -1)
    blocks = v.reshape(v.shape[:-1] + (-1, 32))
    amax = np.abs(blocks).max(-1, keepdims=True)
    byte = np.maximum(np.where(amax > 0, np.frexp(amax)[1] - 1 + 127, 0) - down, 1)
    scale = np.exp2(byte - 127.0)
    codes = (blocks / scale).astype(np.float32).astype(dtype).astype(np.float64)
    return np.moveaxis((codes * scale).reshape(v.shape), -1, axis)


WIDE = False


def mx_kscale(k):
    if not WIDE:
        return np.ones(k)
    levels = np.array([30, -30])
    if k % 512:
        return np.exp2(np.random.permutation(np.resize(levels, k // 32))).repeat(32)
    a = np.empty((k // 512, 16))
    for p in range(k // 512):
        a[p, :8] = np.random.permutation(np.resize(levels, 8))
        for g in range(8):
            far = levels[np.abs(levels - a[p, g]) >= 10]
            a[p, g + 8] = far[np.random.randint(len(far))]
    return np.exp2(a.ravel()).repeat(32)


BF16 = ml_dtypes.bfloat16


def bf(x):
    return np.asarray(x, np.float32).astype(BF16)


def f64(x):
    return np.asarray(x).astype(np.float64)


E2M1 = np.array([0.0, 0.5, 1.0, 1.5, 2.0, 3.0, 4.0, 6.0, -0.0, -0.5, -1.0, -1.5, -2.0, -3.0, -4.0, -6.0])


def pack_weight(w, fmt):
    k, n = w.shape
    w = f64(bf(w)).reshape(k // 32, 32, n)
    amax = np.abs(w).max(1)
    if fmt == "e4m3":
        byte = np.frexp(amax)[1] - 1 + 127 - 7
    else:
        mant, ex = np.frexp(amax / 6.0)
        byte = np.where(mant > 0.5, ex, ex - 1) + 127
    byte = np.clip(np.where(amax > 0, byte, 1), 1, 254)
    scaled = (w * np.exp2(127.0 - byte)[:, None, :]).reshape(k, n).astype(np.float32)
    by_word = np.ascontiguousarray(scaled.reshape(k // 512, 128, 4, n).transpose(0, 1, 3, 2))
    if fmt == "e4m3":
        words = by_word.astype(ml_dtypes.float8_e4m3fn).view(np.uint8)
    else:
        c = by_word.astype(ml_dtypes.float4_e2m1fn).view(np.uint8) & 0xF
        words = c[..., 0::2] | (c[..., 1::2] << 4)
    return np.ascontiguousarray(words), np.ascontiguousarray(byte.astype(np.uint8).reshape(k // 512, 16, n))


def unpack_weight(words, scales, fmt):
    g, p, n, _ = words.shape
    if fmt == "e4m3":
        vals = np.ascontiguousarray(words).view(ml_dtypes.float8_e4m3fn).astype(np.float64)
    else:
        nib = np.empty((g, p, n, 4), np.uint8)
        nib[..., 0::2] = words & 0xF
        nib[..., 1::2] = words >> 4
        vals = E2M1[nib]
    vals = vals * np.repeat(np.exp2(scales.astype(np.float64) - 127.0), 8, axis=1)[..., None]
    return vals.transpose(0, 1, 3, 2).reshape(g * 512, n)

def pack4(w):
    words, scales = pack_weight(w, "e2m1")
    return words.reshape(words.shape[0], 128, -1), scales


def unpack4(words, scales):
    return unpack_weight(words.reshape(words.shape[0], 128, -1, 2), scales, "e2m1")


B, T, D, H, HD, Q_STRIDE, WINDOW, QKV = 1, 1536, 1024, 16, 64, 4, 128, 3
NW = T // (Q_STRIDE * WINDOW)
SEQ = T // NW


def setup_inputs():
    s = mx_kscale(D)
    embeddings = bf(np.random.standard_normal((B, T, D)) * s)
    qkv_w = np.random.standard_normal((QKV * D, D)) / np.sqrt(D) / s[None, :]
    words, scales = pack4(np.ascontiguousarray(qkv_w.T))
    qkv_b = bf(np.random.standard_normal(QKV * D) * 0.3)
    return {"embeddings": embeddings,
            "qkv_w_words": words,
            "qkv_w_scales": scales,
            "qkv_b": qkv_b}


def reference(embeddings, qkv_w_words, qkv_w_scales, qkv_b):
    y = (mxq(f64(embeddings), 2, "e5m2") @ unpack4(qkv_w_words, qkv_w_scales)) + f64(qkv_b)
    qkv = y.reshape(B, SEQ, NW, QKV, H, HD)
    qkv = qkv.transpose(3, 0, 4, 2, 1, 5)
    q, k, v = qkv[0], qkv[1], qkv[2]
    q = q.reshape(B, H, NW, Q_STRIDE, SEQ // Q_STRIDE, HD).max(axis=3)
    return q, k, v

@@ -1,0 +1,245 @@
+from contextlib import ExitStack
+
+import concourse.mybir as mybir
+from concourse.masks import make_identity
+
+T, D, HEADS, HD = 1536, 1024, 16, 64
+WINDOWS = 3
+FLOPS = 2 * T * D * 3 * D
+
+F32 = mybir.dt.float32
+BF16 = mybir.dt.bfloat16
+I32 = mybir.dt.int32
+U32 = mybir.dt.uint32
+U8 = mybir.dt.uint8
+E5M2X4 = mybir.dt.float8_e5m2_x4
+E2M1X4 = mybir.dt.float4_e2m1fn_x4
+ALU = mybir.AluOpType
+
+P = 128
+PASSES = 2
+TILES = 4
+CHUNK = 512
+CHUNK_HEADS = CHUNK // HD
+QUAD = 32
+Q_CHUNKS, K_CHUNKS, V_CHUNKS = (0, 1), (2, 3), (4, 5)
+ACC_BANKS = 6
+TRANSPOSE_BANKS = 2
+
+
+def tile_hieramaskunitattention_pa_kernel(tc, embeddings, qkv_w_words, qkv_w_scales, qkv_b, out_0, out_1, out_2):
+    nc = tc.nc
+    x_rows = embeddings[0].rearrange("(p j w) d -> p j w d", j=TILES, w=WINDOWS)
+
+    with ExitStack() as ctx:
+        keep = ctx.enter_context(tc.tile_pool(name="keep", bufs=1))
+        stage = ctx.enter_context(tc.tile_pool(name="stage", bufs=4))
+        psum = ctx.enter_context(tc.psum_pool(name="psum", bufs=1))
+        ctx.enter_context(tc.manual_schedule())
+
+        ident = keep.tile([P, P], F32, name="ident")
+        select = keep.tile([P, 2], BF16, name="select")
+        bias_rows = keep.tile([P, 3 * CHUNK], BF16, name="bias_rows")
+        w_scales_v = keep.tile([P, PASSES, D], U8, name="w_scales_v", align_bytes=64)
+        w_scales_qk = keep.tile([P, PASSES, 2 * D], U8, name="w_scales_qk", align_bytes=64)
+        kv_codes = [keep.tile([P, TILES, PASSES * P], U32, name="kv_codes%d" % w, align_bytes=64) for w in range(WINDOWS)]
+        kv_scales = [keep.tile([P, TILES, PASSES * P], U8, name="kv_scales%d" % w, align_bytes=64) for w in range(WINDOWS)]
+        q_codes = [keep.tile([P, TILES, PASSES * P], U32, name="q_codes%d" % w, align_bytes=64) for w in range(WINDOWS)]
+        q_scales = [keep.tile([P, TILES, PASSES * P], U8, name="q_scales%d" % w, align_bytes=64) for w in range(WINDOWS)]
+
+        nc.vector.memset(bias_rows[:].bitcast(I32), 0)
+        nc.vector.memset(w_scales_v[:].rearrange("p g n -> p (g n)").bitcast(I32), 0)
+        nc.vector.memset(w_scales_qk[:].rearrange("p g n -> p (g n)").bitcast(I32), 0)
+        nc.gpsimd.memset(select[:], 0.0)
+        nc.gpsimd.memset(select[0:64, 0:1], 1.0)
+        nc.gpsimd.memset(select[64:128, 1:2], 1.0)
+        make_identity(nc, ident[:])
+        for w in range(WINDOWS):
+            nc.gpsimd.memset(kv_scales[w][:].rearrange("p j n -> p (j n)").bitcast(I32), 0)
+
+        x_tiles = {}
+        w_words = {}
+        bias = {}
+        grouped = {}
+        results = {}
+
+        def load_x(w, j0, count):
+            t = keep.tile([P, count, D], BF16, name="x%d_%d" % (w, j0))
+            nc.sync.dma_start(out=t[:], in_=x_rows[:, j0 : j0 + count, w, :])
+            for j in range(count):
+                x_tiles[w, j0 + j] = t[:, j, :]
+
+        def load_words(c):
+            t = keep.tile([P, PASSES, 2 * CHUNK], U8, name="w_words%d" % c, align_bytes=64)
+            src = qkv_w_words[:, :, 2 * CHUNK * c : 2 * CHUNK * (c + 1)].rearrange("g p n -> p g n")
+            nc.sync.dma_start(out=t[:].bitcast(I32), in_=src.bitcast(I32))
+            w_words[c] = t
+
+        def load_scales(plane, n0, n1):
+            for quad in range(4):
+                src = qkv_w_scales[:, 4 * quad : 4 * quad + 4, n0:n1].rearrange("g r n -> r g n")
+                nc.sync.dma_start(out=plane[QUAD * quad : QUAD * quad + 4, :, :].bitcast(I32), in_=src.bitcast(I32))
+
+        def w_scale(c, g):
+            if c in V_CHUNKS:
+                return w_scales_v[:, g, CHUNK * c - 2 * D : CHUNK * (c + 1) - 2 * D]
+            return w_scales_qk[:, g, CHUNK * c : CHUNK * (c + 1)]
+
+        load_x(0, 0, 1)
+        nc.scalar.dma_start(out=bias_rows[0:P:64, :], in_=qkv_b.rearrange("(r n) -> r n", r=2))
+        load_x(0, 1, 1)
+        load_scales(w_scales_v, 2 * D, 3 * D)
+        load_words(V_CHUNKS[0])
+        load_x(0, 2, 2)
+        load_words(V_CHUNKS[1])
+        load_scales(w_scales_qk, 0, 2 * D)
+        load_words(K_CHUNKS[0])
+        load_words(K_CHUNKS[1])
+        load_x(1, 0, 2)
+        load_x(1, 2, 2)
+        load_words(Q_CHUNKS[0])
+        load_words(Q_CHUNKS[1])
+        load_x(2, 0, 2)
+        load_x(2, 2, 2)
+
+        def spread_bias(chunks):
+            bank = psum.tile([P, 2, CHUNK], BF16, name="bias_bank", tag="acc", bufs=ACC_BANKS)
+            for i, c in enumerate(chunks):
+                nc.tensor.matmul(
+                    out=bank[:, i, :],
+                    lhsT=select[:, c // 3 : c // 3 + 1].to_broadcast([P, P]),
+                    rhs=bias_rows[:, CHUNK * (c % 3) : CHUNK * (c % 3 + 1)],
+                    start=True,
+                    stop=True,
+                )
+            return bank
+
+        def keep_bias(chunks, bank, copy):
+            t = keep.tile([P, 2, CHUNK], BF16, name="bias%d" % chunks[0])
+            copy(out=t[:], in_=bank[:])
+            for i, c in enumerate(chunks):
+                bias[c] = t[:, i, :]
+
+        def transpose_x(w, j):
+            words = x_tiles[w, j].bitcast(F32)
+            bank = psum.tile([P, PASSES, 2, P], F32, name="xt_bank", tag="xt", bufs=TRANSPOSE_BANKS)
+            for g in range(PASSES):
+                for u in range(2):
+                    nc.tensor.transpose(bank[:, g, u, :], words[:, 256 * g + u : 256 * (g + 1) : 2], ident[:])
+            t = stage.tile([P, PASSES * P * 4], BF16, name="grouped", align_bytes=64)
+            nc.scalar.copy(
+                out=t[:].bitcast(F32).rearrange("p (g r u) -> p g r u", g=PASSES, u=2),
+                in_=bank[:].rearrange("p g u r -> p g r u"),
+            )
+            grouped[w, j] = t
+
+        def quantize(w, j):
+            nc.vector.quantize_mx(out=kv_codes[w][:, j, :].bitcast(E5M2X4), scales=kv_scales[w][:, j, :], in_=grouped[w, j][:])
+
+        def regroup_for_q(w):
+            for src, dst in ((kv_codes[w][:], q_codes[w][:]), (kv_scales[w][:].bitcast(U32), q_scales[w][:].bitcast(U32))):
+                half = src.shape[2] // PASSES
+                for g in range(PASSES):
+                    cols = slice(g * half, (g + 1) * half)
+                    nc.scalar.copy(
+                        out=dst[:, :, cols].rearrange("p m (j a) -> p m j a", j=TILES),
+                        in_=src[:, :, cols].rearrange("p j (m a) -> p m j a", m=TILES),
+                    )
+
+        def multiply(codes, scales, j, c):
+            bank = psum.tile([P, CHUNK], F32, name="acc_bank", tag="acc", bufs=ACC_BANKS)
+            for g in range(PASSES):
+                nc.tensor.matmul_mx(
+                    out=bank[:],
+                    lhsT=codes[:, j, P * g : P * (g + 1)].bitcast(E5M2X4),
+                    lhsT_scale=scales[:, j, P * g : P * (g + 1)],
+                    rhs=w_words[c][:, g, :].bitcast(E2M1X4),
+                    rhs_scale=w_scale(c, g),
+                    start=(g == 0),
+                    stop=(g == PASSES - 1),
+                )
+            return bank
+
+        def key_value(w, c, j):
+            bank = multiply(kv_codes[w], kv_scales[w], j, c)
+            if j == 0:
+                results[w, c] = keep.tile([P, CHUNK_HEADS, TILES, HD], F32, name="kv%d_%d" % (w, c))
+            t = results[w, c]
+            nc.vector.tensor_tensor(
+                out=t[:, :, j, :],
+                in0=bank[:].rearrange("p (h d) -> p h d", d=HD),
+                in1=bias[c].rearrange("p (h d) -> p h d", d=HD),
+                op=ALU.add,
+            )
+            if j == TILES - 1:
+                out = out_1 if c in K_CHUNKS else out_2
+                h0 = CHUNK_HEADS * (c % 2)
+                dst = out[0, h0 : h0 + CHUNK_HEADS, w].rearrange("h (p j) d -> p h (j d)", j=TILES)
+                nc.sync.dma_start(out=dst, in_=t[:].rearrange("p h j d -> p h (j d)"))
+
+        def query(w, c, m):
+            bank = multiply(q_codes[w], q_scales[w], m, c)
+            if m == 0:
+                results[w, c] = keep.tile([P, CHUNK], F32, name="q%d_%d" % (w, c))
+                nc.scalar.copy(out=results[w, c][:], in_=bank[:])
+            else:
+                nc.vector.tensor_tensor(out=results[w, c][:], in0=bank[:], in1=results[w, c][:], op=ALU.max)
+
+        def finish_query(w, c):
+            t = results[w, c]
+            nc.vector.tensor_tensor(out=t[:], in0=t[:], in1=bias[c], op=ALU.add)
+            h0 = CHUNK_HEADS * c
+            dst = out_0[0, h0 : h0 + CHUNK_HEADS, w].rearrange("h (a j) d -> j a h d", j=TILES)
+            for j in range(TILES):
+                nc.sync.dma_start(out=dst[j], in_=t[QUAD * j : QUAD * (j + 1), :].rearrange("p (h d) -> p h d", d=HD))
+
+        keep_bias(V_CHUNKS, spread_bias(V_CHUNKS), nc.vector.tensor_copy)
+        transpose_x(0, 0)
+        transpose_x(0, 1)
+        k_bias_bank = spread_bias(K_CHUNKS)
+        quantize(0, 0)
+        quantize(0, 1)
+        key_value(0, V_CHUNKS[0], 0)
+        transpose_x(0, 2)
+        transpose_x(0, 3)
+        q_bias_bank = spread_bias(Q_CHUNKS)
+        keep_bias(K_CHUNKS, k_bias_bank, nc.scalar.copy)
+        keep_bias(Q_CHUNKS, q_bias_bank, nc.scalar.copy)
+        quantize(0, 2)
+        key_value(0, V_CHUNKS[0], 1)
+        quantize(0, 3)
+        regroup_for_q(0)
+        key_value(0, V_CHUNKS[1], 0)
+        key_value(0, V_CHUNKS[1], 1)
+        for c in V_CHUNKS:
+            for j in (2, 3):
+                key_value(0, c, j)
+
+        for w in range(WINDOWS):
+            more = w + 1 < WINDOWS
+            if w > 0:
+                for c in V_CHUNKS:
+                    for j in range(TILES):
+                        key_value(w, c, j)
+            for j in range(TILES):
+                key_value(w, K_CHUNKS[0], j)
+            if more:
+                transpose_x(w + 1, 0)
+                transpose_x(w + 1, 1)
+                quantize(w + 1, 0)
+            for j in range(TILES):
+                key_value(w, K_CHUNKS[1], j)
+                if more and j == 0:
+                    quantize(w + 1, 1)
+            if more:
+                transpose_x(w + 1, 2)
+                transpose_x(w + 1, 3)
+                quantize(w + 1, 2)
+                quantize(w + 1, 3)
+            for m in range(TILES):
+                for c in Q_CHUNKS:
+                    query(w, c, m)
+                if more and m == 0:
+                    regroup_for_q(w + 1)
+            for c in Q_CHUNKS:
+                finish_query(w, c)

@@ -23,8 +23,10 @@ CHUNK = 512
 CHUNK_HEADS = CHUNK // HD
 QUAD = 32
 Q_CHUNKS, K_CHUNKS, V_CHUNKS = (0, 1), (2, 3), (4, 5)
-ACC_BANKS = 6
-TRANSPOSE_BANKS = 2
+BANKS = 8
+HALF = CHUNK // 2
+BIAS_ROWS = 4
+BIAS_ROW = 3 * D // BIAS_ROWS
 
 
 def tile_hieramaskunitattention_pa_kernel(tc, embeddings, qkv_w_words, qkv_w_scales, qkv_b, out_0, out_1, out_2):
@@ -38,8 +40,8 @@ def tile_hieramaskunitattention_pa_kernel(tc, embeddings, qkv_w_words, qkv_w_sca
         ctx.enter_context(tc.manual_schedule())
 
         ident = keep.tile([P, P], F32, name="ident")
-        select = keep.tile([P, 2], BF16, name="select")
-        bias_rows = keep.tile([P, 3 * CHUNK], BF16, name="bias_rows")
+        select = keep.tile([P, BIAS_ROWS], BF16, name="select")
+        bias_rows = keep.tile([P, BIAS_ROW], BF16, name="bias_rows")
         w_scales_v = keep.tile([P, PASSES, D], U8, name="w_scales_v", align_bytes=64)
         w_scales_qk = keep.tile([P, PASSES, 2 * D], U8, name="w_scales_qk", align_bytes=64)
         kv_codes = [keep.tile([P, TILES, PASSES * P], U32, name="kv_codes%d" % w, align_bytes=64) for w in range(WINDOWS)]
@@ -47,17 +49,19 @@ def tile_hieramaskunitattention_pa_kernel(tc, embeddings, qkv_w_words, qkv_w_sca
         q_codes = [keep.tile([P, TILES, PASSES * P], U32, name="q_codes%d" % w, align_bytes=64) for w in range(WINDOWS)]
         q_scales = [keep.tile([P, TILES, PASSES * P], U8, name="q_scales%d" % w, align_bytes=64) for w in range(WINDOWS)]
 
-        nc.vector.memset(bias_rows[:].bitcast(I32), 0)
+        nc.gpsimd.memset(bias_rows[:].bitcast(I32), 0)
         nc.vector.memset(w_scales_v[:].rearrange("p g n -> p (g n)").bitcast(I32), 0)
         nc.vector.memset(w_scales_qk[:].rearrange("p g n -> p (g n)").bitcast(I32), 0)
         nc.gpsimd.memset(select[:], 0.0)
-        nc.gpsimd.memset(select[0:64, 0:1], 1.0)
-        nc.gpsimd.memset(select[64:128, 1:2], 1.0)
+        for r in range(BIAS_ROWS):
+            nc.gpsimd.memset(select[QUAD * r : QUAD * (r + 1), r : r + 1], 1.0)
         make_identity(nc, ident[:])
         for w in range(WINDOWS):
             nc.gpsimd.memset(kv_scales[w][:].rearrange("p j n -> p (j n)").bitcast(I32), 0)
 
         x_tiles = {}
+        x_pairs = {}
+        x_split = {}
         w_words = {}
         bias = {}
         grouped = {}
@@ -66,6 +70,7 @@ def tile_hieramaskunitattention_pa_kernel(tc, embeddings, qkv_w_words, qkv_w_sca
         def load_x(w, j0, count):
             t = keep.tile([P, count, D], BF16, name="x%d_%d" % (w, j0))
             nc.sync.dma_start(out=t[:], in_=x_rows[:, j0 : j0 + count, w, :])
+            x_pairs[w, j0] = t[:]
             for j in range(count):
                 x_tiles[w, j0 + j] = t[:, j, :]
 
@@ -86,7 +91,7 @@ def tile_hieramaskunitattention_pa_kernel(tc, embeddings, qkv_w_words, qkv_w_sca
             return w_scales_qk[:, g, CHUNK * c : CHUNK * (c + 1)]
 
         load_x(0, 0, 1)
-        nc.scalar.dma_start(out=bias_rows[0:P:64, :], in_=qkv_b.rearrange("(r n) -> r n", r=2))
+        nc.scalar.dma_start(out=bias_rows[0:P:QUAD, :], in_=qkv_b.rearrange("(r n) -> r n", r=BIAS_ROWS))
         load_x(0, 1, 1)
         load_scales(w_scales_v, 2 * D, 3 * D)
         load_words(V_CHUNKS[0])
@@ -103,29 +108,42 @@ def tile_hieramaskunitattention_pa_kernel(tc, embeddings, qkv_w_words, qkv_w_sca
         load_x(2, 2, 2)
 
         def spread_bias(chunks):
-            bank = psum.tile([P, 2, CHUNK], BF16, name="bias_bank", tag="acc", bufs=ACC_BANKS)
-            for i, c in enumerate(chunks):
+            bank = psum.tile([P, 2 * CHUNK], BF16, name="bias_bank", tag="bank", bufs=BANKS)
+            for n0 in range(0, 2 * CHUNK, HALF):
+                row, col = divmod(CHUNK * chunks[0] + n0, BIAS_ROW)
                 nc.tensor.matmul(
-                    out=bank[:, i, :],
-                    lhsT=select[:, c // 3 : c // 3 + 1].to_broadcast([P, P]),
-                    rhs=bias_rows[:, CHUNK * (c % 3) : CHUNK * (c % 3 + 1)],
+                    out=bank[:, n0 : n0 + HALF],
+                    lhsT=select[:, row : row + 1].to_broadcast([P, P]),
+                    rhs=bias_rows[:, col : col + HALF],
                     start=True,
                     stop=True,
                 )
             return bank
 
         def keep_bias(chunks, bank, copy):
-            t = keep.tile([P, 2, CHUNK], BF16, name="bias%d" % chunks[0])
+            t = keep.tile([P, 2 * CHUNK], BF16, name="bias%d" % chunks[0])
             copy(out=t[:], in_=bank[:])
             for i, c in enumerate(chunks):
-                bias[c] = t[:, i, :]
+                bias[c] = t[:, CHUNK * i : CHUNK * (i + 1)]
+
+        def split_words(w, j0):
+            t = keep.tile([P, 2, PASSES, 2, P], F32, name="x_split%d_%d" % (w % 2, j0))
+            nc.scalar.copy(
+                out=t[:].rearrange("p j g u r -> p (j g) u r"),
+                in_=x_pairs[w, j0].rearrange("p j d -> p (j d)").bitcast(F32).rearrange("p (a r u) -> p a u r", u=2, r=P),
+            )
+            for j in range(2):
+                x_split[w, j0 + j] = t[:, j]
 
         def transpose_x(w, j):
-            words = x_tiles[w, j].bitcast(F32)
-            bank = psum.tile([P, PASSES, 2, P], F32, name="xt_bank", tag="xt", bufs=TRANSPOSE_BANKS)
+            bank = psum.tile([P, PASSES, 2, P], F32, name="xt_bank", tag="bank", bufs=BANKS)
             for g in range(PASSES):
                 for u in range(2):
-                    nc.tensor.transpose(bank[:, g, u, :], words[:, 256 * g + u : 256 * (g + 1) : 2], ident[:])
+                    if w == 0:
+                        src = x_tiles[w, j].bitcast(F32)[:, 256 * g + u : 256 * (g + 1) : 2]
+                    else:
+                        src = x_split[w, j][:, g, u, :]
+                    nc.tensor.transpose(bank[:, g, u, :], src, ident[:])
             t = stage.tile([P, PASSES * P * 4], BF16, name="grouped", align_bytes=64)
             nc.scalar.copy(
                 out=t[:].bitcast(F32).rearrange("p (g r u) -> p g r u", g=PASSES, u=2),
@@ -147,7 +165,7 @@ def tile_hieramaskunitattention_pa_kernel(tc, embeddings, qkv_w_words, qkv_w_sca
                     )
 
         def multiply(codes, scales, j, c):
-            bank = psum.tile([P, CHUNK], F32, name="acc_bank", tag="acc", bufs=ACC_BANKS)
+            bank = psum.tile([P, CHUNK], F32, name="acc_bank", tag="bank", bufs=BANKS)
             for g in range(PASSES):
                 nc.tensor.matmul_mx(
                     out=bank[:],
@@ -183,11 +201,17 @@ def tile_hieramaskunitattention_pa_kernel(tc, embeddings, qkv_w_words, qkv_w_sca
                 results[w, c] = keep.tile([P, CHUNK], F32, name="q%d_%d" % (w, c))
                 nc.scalar.copy(out=results[w, c][:], in_=bank[:])
             else:
-                nc.vector.tensor_tensor(out=results[w, c][:], in0=bank[:], in1=results[w, c][:], op=ALU.max)
+                for n0 in (0, HALF):
+                    t = results[w, c][:, n0 : n0 + HALF]
+                    nc.vector.tensor_tensor(out=t, in0=bank[:, n0 : n0 + HALF], in1=t, op=ALU.max)
 
         def finish_query(w, c):
             t = results[w, c]
-            nc.vector.tensor_tensor(out=t[:], in0=t[:], in1=bias[c], op=ALU.add)
+            if (w, c) == (WINDOWS - 1, Q_CHUNKS[-1]):
+                for n0 in (0, HALF):
+                    nc.vector.tensor_tensor(out=t[:, n0 : n0 + HALF], in0=t[:, n0 : n0 + HALF], in1=bias[c][:, n0 : n0 + HALF], op=ALU.add)
+            else:
+                nc.gpsimd.tensor_tensor(out=t[:], in0=t[:], in1=bias[c], op=ALU.add)
             h0 = CHUNK_HEADS * c
             dst = out_0[0, h0 : h0 + CHUNK_HEADS, w].rearrange("h (a j) d -> j a h d", j=TILES)
             for j in range(TILES):
@@ -196,20 +220,18 @@ def tile_hieramaskunitattention_pa_kernel(tc, embeddings, qkv_w_words, qkv_w_sca
         keep_bias(V_CHUNKS, spread_bias(V_CHUNKS), nc.vector.tensor_copy)
         transpose_x(0, 0)
         transpose_x(0, 1)
-        k_bias_bank = spread_bias(K_CHUNKS)
+        keep_bias(K_CHUNKS, spread_bias(K_CHUNKS), nc.scalar.copy)
+        keep_bias(Q_CHUNKS, spread_bias(Q_CHUNKS), nc.scalar.copy)
         quantize(0, 0)
         quantize(0, 1)
         key_value(0, V_CHUNKS[0], 0)
         transpose_x(0, 2)
         transpose_x(0, 3)
-        q_bias_bank = spread_bias(Q_CHUNKS)
-        keep_bias(K_CHUNKS, k_bias_bank, nc.scalar.copy)
-        keep_bias(Q_CHUNKS, q_bias_bank, nc.scalar.copy)
-        quantize(0, 2)
         key_value(0, V_CHUNKS[0], 1)
+        quantize(0, 2)
+        key_value(0, V_CHUNKS[1], 0)
         quantize(0, 3)
         regroup_for_q(0)
-        key_value(0, V_CHUNKS[1], 0)
         key_value(0, V_CHUNKS[1], 1)
         for c in V_CHUNKS:
             for j in (2, 3):
@@ -217,29 +239,22 @@ def tile_hieramaskunitattention_pa_kernel(tc, embeddings, qkv_w_words, qkv_w_sca
 
         for w in range(WINDOWS):
             more = w + 1 < WINDOWS
-            if w > 0:
-                for c in V_CHUNKS:
-                    for j in range(TILES):
-                        key_value(w, c, j)
-            for j in range(TILES):
-                key_value(w, K_CHUNKS[0], j)
             if more:
-                transpose_x(w + 1, 0)
-                transpose_x(w + 1, 1)
-                quantize(w + 1, 0)
-            for j in range(TILES):
-                key_value(w, K_CHUNKS[1], j)
-                if more and j == 0:
-                    quantize(w + 1, 1)
+                split_words(w + 1, 0)
+                split_words(w + 1, 2)
+            for c in (V_CHUNKS if w > 0 else ()) + K_CHUNKS:
+                for j in range(TILES):
+                    key_value(w, c, j)
             if more:
-                transpose_x(w + 1, 2)
-                transpose_x(w + 1, 3)
-                quantize(w + 1, 2)
-                quantize(w + 1, 3)
-            for m in range(TILES):
-                for c in Q_CHUNKS:
-                    query(w, c, m)
-                if more and m == 0:
-                    regroup_for_q(w + 1)
+                for j in range(TILES):
+                    transpose_x(w + 1, j)
+                for j in range(TILES):
+                    quantize(w + 1, j)
             for c in Q_CHUNKS:
+                query(w, c, 0)
+            for c in Q_CHUNKS:
+                for m in range(1, TILES):
+                    query(w, c, m)
                 finish_query(w, c)
+            if more:
+                regroup_for_q(w + 1)

@@ -46,8 +46,8 @@ def tile_hieramaskunitattention_pa_kernel(tc, embeddings, qkv_w_words, qkv_w_sca
         w_scales_qk = keep.tile([P, PASSES, 2 * D], U8, name="w_scales_qk", align_bytes=64)
         kv_codes = [keep.tile([P, TILES, PASSES * P], U32, name="kv_codes%d" % w, align_bytes=64) for w in range(WINDOWS)]
         kv_scales = [keep.tile([P, TILES, PASSES * P], U8, name="kv_scales%d" % w, align_bytes=64) for w in range(WINDOWS)]
-        q_codes = [keep.tile([P, TILES, PASSES * P], U32, name="q_codes%d" % w, align_bytes=64) for w in range(WINDOWS)]
-        q_scales = [keep.tile([P, TILES, PASSES * P], U8, name="q_scales%d" % w, align_bytes=64) for w in range(WINDOWS)]
+        q_codes = [keep.tile([P, PASSES * TILES * P], U32, name="q_codes%d" % w, align_bytes=64) for w in range(WINDOWS)]
+        q_scales = [keep.tile([P, PASSES * TILES * P], U8, name="q_scales%d" % w, align_bytes=64) for w in range(WINDOWS)]
 
         nc.gpsimd.memset(bias_rows[:].bitcast(I32), 0)
         nc.vector.memset(w_scales_v[:].rearrange("p g n -> p (g n)").bitcast(I32), 0)
@@ -81,9 +81,9 @@ def tile_hieramaskunitattention_pa_kernel(tc, embeddings, qkv_w_words, qkv_w_sca
             w_words[c] = t
 
         def load_scales(plane, n0, n1):
-            for quad in range(4):
-                src = qkv_w_scales[:, 4 * quad : 4 * quad + 4, n0:n1].rearrange("g r n -> r g n")
-                nc.sync.dma_start(out=plane[QUAD * quad : QUAD * quad + 4, :, :].bitcast(I32), in_=src.bitcast(I32))
+            for r in range(4):
+                src = qkv_w_scales[:, r:16:4, n0:n1].rearrange("g q n -> q g n")
+                nc.sync.dma_start(out=plane[r:P:QUAD, :, :].bitcast(I32), in_=src.bitcast(I32))
 
         def w_scale(c, g):
             if c in V_CHUNKS:
@@ -154,23 +154,17 @@ def tile_hieramaskunitattention_pa_kernel(tc, embeddings, qkv_w_words, qkv_w_sca
         def quantize(w, j):
             nc.vector.quantize_mx(out=kv_codes[w][:, j, :].bitcast(E5M2X4), scales=kv_scales[w][:, j, :], in_=grouped[w, j][:])
 
-        def regroup_for_q(w):
-            for src, dst in ((kv_codes[w][:], q_codes[w][:]), (kv_scales[w][:].bitcast(U32), q_scales[w][:].bitcast(U32))):
-                half = src.shape[2] // PASSES
-                for g in range(PASSES):
-                    cols = slice(g * half, (g + 1) * half)
-                    nc.scalar.copy(
-                        out=dst[:, :, cols].rearrange("p m (j a) -> p m j a", j=TILES),
-                        in_=src[:, :, cols].rearrange("p j (m a) -> p m j a", m=TILES),
-                    )
+        def regroup_for_q(copy, src, dst):
+            copy(out=dst[:].rearrange("p (n j) -> p n j", j=TILES), in_=src[:].rearrange("p j n -> p n j"))
 
-        def multiply(codes, scales, j, c):
+        def multiply(operand, c):
             bank = psum.tile([P, CHUNK], F32, name="acc_bank", tag="bank", bufs=BANKS)
             for g in range(PASSES):
+                codes, scales = operand(g)
                 nc.tensor.matmul_mx(
                     out=bank[:],
-                    lhsT=codes[:, j, P * g : P * (g + 1)].bitcast(E5M2X4),
-                    lhsT_scale=scales[:, j, P * g : P * (g + 1)],
+                    lhsT=codes.bitcast(E5M2X4),
+                    lhsT_scale=scales,
                     rhs=w_words[c][:, g, :].bitcast(E2M1X4),
                     rhs_scale=w_scale(c, g),
                     start=(g == 0),
@@ -179,7 +173,7 @@ def tile_hieramaskunitattention_pa_kernel(tc, embeddings, qkv_w_words, qkv_w_sca
             return bank
 
         def key_value(w, c, j):
-            bank = multiply(kv_codes[w], kv_scales[w], j, c)
+            bank = multiply(lambda g: (kv_codes[w][:, j, P * g : P * (g + 1)], kv_scales[w][:, j, P * g : P * (g + 1)]), c)
             if j == 0:
                 results[w, c] = keep.tile([P, CHUNK_HEADS, TILES, HD], F32, name="kv%d_%d" % (w, c))
             t = results[w, c]
@@ -196,7 +190,8 @@ def tile_hieramaskunitattention_pa_kernel(tc, embeddings, qkv_w_words, qkv_w_sca
                 nc.sync.dma_start(out=dst, in_=t[:].rearrange("p h j d -> p h (j d)"))
 
         def query(w, c, m):
-            bank = multiply(q_codes[w], q_scales[w], m, c)
+            cols = [slice(P * (TILES * g + m), P * (TILES * g + m + 1)) for g in range(PASSES)]
+            bank = multiply(lambda g: (q_codes[w][:, cols[g]], q_scales[w][:, cols[g]]), c)
             if m == 0:
                 results[w, c] = keep.tile([P, CHUNK], F32, name="q%d_%d" % (w, c))
                 nc.scalar.copy(out=results[w, c][:], in_=bank[:])
@@ -213,9 +208,8 @@ def tile_hieramaskunitattention_pa_kernel(tc, embeddings, qkv_w_words, qkv_w_sca
             else:
                 nc.gpsimd.tensor_tensor(out=t[:], in0=t[:], in1=bias[c], op=ALU.add)
             h0 = CHUNK_HEADS * c
-            dst = out_0[0, h0 : h0 + CHUNK_HEADS, w].rearrange("h (a j) d -> j a h d", j=TILES)
-            for j in range(TILES):
-                nc.sync.dma_start(out=dst[j], in_=t[QUAD * j : QUAD * (j + 1), :].rearrange("p (h d) -> p h d", d=HD))
+            dst = out_0[0, h0 : h0 + CHUNK_HEADS, w].rearrange("h i d -> i h d")
+            nc.sync.dma_start(out=dst, in_=t[:].rearrange("p (h d) -> p h d", d=HD))
 
         keep_bias(V_CHUNKS, spread_bias(V_CHUNKS), nc.vector.tensor_copy)
         transpose_x(0, 0)
@@ -231,7 +225,8 @@ def tile_hieramaskunitattention_pa_kernel(tc, embeddings, qkv_w_words, qkv_w_sca
         quantize(0, 2)
         key_value(0, V_CHUNKS[1], 0)
         quantize(0, 3)
-        regroup_for_q(0)
+        regroup_for_q(nc.gpsimd.tensor_copy, kv_scales[0], q_scales[0])
+        regroup_for_q(nc.scalar.copy, kv_codes[0], q_codes[0])
         key_value(0, V_CHUNKS[1], 1)
         for c in V_CHUNKS:
             for j in (2, 3):
@@ -250,6 +245,7 @@ def tile_hieramaskunitattention_pa_kernel(tc, embeddings, qkv_w_words, qkv_w_sca
                     transpose_x(w + 1, j)
                 for j in range(TILES):
                     quantize(w + 1, j)
+                regroup_for_q(nc.gpsimd.tensor_copy, kv_scales[w + 1], q_scales[w + 1])
             for c in Q_CHUNKS:
                 query(w, c, 0)
             for c in Q_CHUNKS:
@@ -257,4 +253,4 @@ def tile_hieramaskunitattention_pa_kernel(tc, embeddings, qkv_w_words, qkv_w_sca
                     query(w, c, m)
                 finish_query(w, c)
             if more:
-                regroup_for_q(w + 1)
+                regroup_for_q(nc.scalar.copy, kv_codes[w + 1], q_codes[w + 1])

from contextlib import ExitStack

import concourse.mybir as mybir
from concourse.masks import make_identity

T, D, HEADS, HD = 1536, 1024, 16, 64
WINDOWS = 3
FLOPS = 2 * T * D * 3 * D

F32 = mybir.dt.float32
BF16 = mybir.dt.bfloat16
I32 = mybir.dt.int32
U32 = mybir.dt.uint32
U8 = mybir.dt.uint8
E5M2X4 = mybir.dt.float8_e5m2_x4
E2M1X4 = mybir.dt.float4_e2m1fn_x4
ALU = mybir.AluOpType

P = 128
PASSES = 2
TILES = 4
CHUNK = 512
CHUNK_HEADS = CHUNK // HD
QUAD = 32
Q_CHUNKS, K_CHUNKS, V_CHUNKS = (0, 1), (2, 3), (4, 5)
BANKS = 8
HALF = CHUNK // 2
BIAS_ROWS = 4
BIAS_ROW = 3 * D // BIAS_ROWS


def tile_hieramaskunitattention_pa_kernel(tc, embeddings, qkv_w_words, qkv_w_scales, qkv_b, out_0, out_1, out_2):
    nc = tc.nc
    x_rows = embeddings[0].rearrange("(p j w) d -> p j w d", j=TILES, w=WINDOWS)

    with ExitStack() as ctx:
        keep = ctx.enter_context(tc.tile_pool(name="keep", bufs=1))
        stage = ctx.enter_context(tc.tile_pool(name="stage", bufs=4))
        psum = ctx.enter_context(tc.psum_pool(name="psum", bufs=1))
        ctx.enter_context(tc.manual_schedule())

        ident = keep.tile([P, P], F32, name="ident")
        select = keep.tile([P, BIAS_ROWS], BF16, name="select")
        bias_rows = keep.tile([P, BIAS_ROW], BF16, name="bias_rows")
        w_scales_v = keep.tile([P, PASSES, D], U8, name="w_scales_v", align_bytes=64)
        w_scales_qk = keep.tile([P, PASSES, 2 * D], U8, name="w_scales_qk", align_bytes=64)
        kv_codes = [keep.tile([P, TILES, PASSES * P], U32, name="kv_codes%d" % w, align_bytes=64) for w in range(WINDOWS)]
        kv_scales = [keep.tile([P, TILES, PASSES * P], U8, name="kv_scales%d" % w, align_bytes=64) for w in range(WINDOWS)]
        q_codes = [keep.tile([P, PASSES * TILES * P], U32, name="q_codes%d" % w, align_bytes=64) for w in range(WINDOWS)]
        q_scales = [keep.tile([P, PASSES * TILES * P], U8, name="q_scales%d" % w, align_bytes=64) for w in range(WINDOWS)]

        nc.gpsimd.memset(bias_rows[:].bitcast(I32), 0)
        nc.vector.memset(w_scales_v[:].rearrange("p g n -> p (g n)").bitcast(I32), 0)
        nc.vector.memset(w_scales_qk[:].rearrange("p g n -> p (g n)").bitcast(I32), 0)
        nc.gpsimd.memset(select[:], 0.0)
        for r in range(BIAS_ROWS):
            nc.gpsimd.memset(select[QUAD * r : QUAD * (r + 1), r : r + 1], 1.0)
        make_identity(nc, ident[:])
        for w in range(WINDOWS):
            nc.gpsimd.memset(kv_scales[w][:].rearrange("p j n -> p (j n)").bitcast(I32), 0)

        x_tiles = {}
        x_pairs = {}
        x_split = {}
        w_words = {}
        bias = {}
        grouped = {}
        results = {}

        def load_x(w, j0, count):
            t = keep.tile([P, count, D], BF16, name="x%d_%d" % (w, j0))
            nc.sync.dma_start(out=t[:], in_=x_rows[:, j0 : j0 + count, w, :])
            x_pairs[w, j0] = t[:]
            for j in range(count):
                x_tiles[w, j0 + j] = t[:, j, :]

        def load_words(c):
            t = keep.tile([P, PASSES, 2 * CHUNK], U8, name="w_words%d" % c, align_bytes=64)
            src = qkv_w_words[:, :, 2 * CHUNK * c : 2 * CHUNK * (c + 1)].rearrange("g p n -> p g n")
            nc.sync.dma_start(out=t[:].bitcast(I32), in_=src.bitcast(I32))
            w_words[c] = t

        def load_scales(plane, n0, n1):
            for r in range(4):
                src = qkv_w_scales[:, r:16:4, n0:n1].rearrange("g q n -> q g n")
                nc.sync.dma_start(out=plane[r:P:QUAD, :, :].bitcast(I32), in_=src.bitcast(I32))

        def w_scale(c, g):
            if c in V_CHUNKS:
                return w_scales_v[:, g, CHUNK * c - 2 * D : CHUNK * (c + 1) - 2 * D]
            return w_scales_qk[:, g, CHUNK * c : CHUNK * (c + 1)]

        load_x(0, 0, 1)
        nc.scalar.dma_start(out=bias_rows[0:P:QUAD, :], in_=qkv_b.rearrange("(r n) -> r n", r=BIAS_ROWS))
        load_x(0, 1, 1)
        load_scales(w_scales_v, 2 * D, 3 * D)
        load_words(V_CHUNKS[0])
        load_x(0, 2, 2)
        load_words(V_CHUNKS[1])
        load_scales(w_scales_qk, 0, 2 * D)
        load_words(K_CHUNKS[0])
        load_words(K_CHUNKS[1])
        load_x(1, 0, 2)
        load_x(1, 2, 2)
        load_words(Q_CHUNKS[0])
        load_words(Q_CHUNKS[1])
        load_x(2, 0, 2)
        load_x(2, 2, 2)

        def spread_bias(chunks):
            bank = psum.tile([P, 2 * CHUNK], BF16, name="bias_bank", tag="bank", bufs=BANKS)
            for n0 in range(0, 2 * CHUNK, HALF):
                row, col = divmod(CHUNK * chunks[0] + n0, BIAS_ROW)
                nc.tensor.matmul(
                    out=bank[:, n0 : n0 + HALF],
                    lhsT=select[:, row : row + 1].to_broadcast([P, P]),
                    rhs=bias_rows[:, col : col + HALF],
                    start=True,
                    stop=True,
                )
            return bank

        def keep_bias(chunks, bank, copy):
            t = keep.tile([P, 2 * CHUNK], BF16, name="bias%d" % chunks[0])
            copy(out=t[:], in_=bank[:])
            for i, c in enumerate(chunks):
                bias[c] = t[:, CHUNK * i : CHUNK * (i + 1)]

        def split_words(w, j0):
            t = keep.tile([P, 2, PASSES, 2, P], F32, name="x_split%d_%d" % (w % 2, j0))
            nc.scalar.copy(
                out=t[:].rearrange("p j g u r -> p (j g) u r"),
                in_=x_pairs[w, j0].rearrange("p j d -> p (j d)").bitcast(F32).rearrange("p (a r u) -> p a u r", u=2, r=P),
            )
            for j in range(2):
                x_split[w, j0 + j] = t[:, j]

        def transpose_x(w, j):
            bank = psum.tile([P, PASSES, 2, P], F32, name="xt_bank", tag="bank", bufs=BANKS)
            for g in range(PASSES):
                for u in range(2):
                    if w == 0:
                        src = x_tiles[w, j].bitcast(F32)[:, 256 * g + u : 256 * (g + 1) : 2]
                    else:
                        src = x_split[w, j][:, g, u, :]
                    nc.tensor.transpose(bank[:, g, u, :], src, ident[:])
            t = stage.tile([P, PASSES * P * 4], BF16, name="grouped", align_bytes=64)
            nc.scalar.copy(
                out=t[:].bitcast(F32).rearrange("p (g r u) -> p g r u", g=PASSES, u=2),
                in_=bank[:].rearrange("p g u r -> p g r u"),
            )
            grouped[w, j] = t

        def quantize(w, j):
            nc.vector.quantize_mx(out=kv_codes[w][:, j, :].bitcast(E5M2X4), scales=kv_scales[w][:, j, :], in_=grouped[w, j][:])

        def regroup_for_q(copy, src, dst):
            copy(out=dst[:].rearrange("p (n j) -> p n j", j=TILES), in_=src[:].rearrange("p j n -> p n j"))

        def multiply(operand, c):
            bank = psum.tile([P, CHUNK], F32, name="acc_bank", tag="bank", bufs=BANKS)
            for g in range(PASSES):
                codes, scales = operand(g)
                nc.tensor.matmul_mx(
                    out=bank[:],
                    lhsT=codes.bitcast(E5M2X4),
                    lhsT_scale=scales,
                    rhs=w_words[c][:, g, :].bitcast(E2M1X4),
                    rhs_scale=w_scale(c, g),
                    start=(g == 0),
                    stop=(g == PASSES - 1),
                )
            return bank

        def key_value(w, c, j):
            bank = multiply(lambda g: (kv_codes[w][:, j, P * g : P * (g + 1)], kv_scales[w][:, j, P * g : P * (g + 1)]), c)
            if j == 0:
                results[w, c] = keep.tile([P, CHUNK_HEADS, TILES, HD], F32, name="kv%d_%d" % (w, c))
            t = results[w, c]
            nc.vector.tensor_tensor(
                out=t[:, :, j, :],
                in0=bank[:].rearrange("p (h d) -> p h d", d=HD),
                in1=bias[c].rearrange("p (h d) -> p h d", d=HD),
                op=ALU.add,
            )
            if j == TILES - 1:
                out = out_1 if c in K_CHUNKS else out_2
                h0 = CHUNK_HEADS * (c % 2)
                dst = out[0, h0 : h0 + CHUNK_HEADS, w].rearrange("h (p j) d -> p h (j d)", j=TILES)
                nc.sync.dma_start(out=dst, in_=t[:].rearrange("p h j d -> p h (j d)"))

        def query(w, c, m):
            cols = [slice(P * (TILES * g + m), P * (TILES * g + m + 1)) for g in range(PASSES)]
            bank = multiply(lambda g: (q_codes[w][:, cols[g]], q_scales[w][:, cols[g]]), c)
            if m == 0:
                results[w, c] = keep.tile([P, CHUNK], F32, name="q%d_%d" % (w, c))
                nc.scalar.copy(out=results[w, c][:], in_=bank[:])
            else:
                for n0 in (0, HALF):
                    t = results[w, c][:, n0 : n0 + HALF]
                    nc.vector.tensor_tensor(out=t, in0=bank[:, n0 : n0 + HALF], in1=t, op=ALU.max)

        def finish_query(w, c):
            t = results[w, c]
            if (w, c) == (WINDOWS - 1, Q_CHUNKS[-1]):
                for n0 in (0, HALF):
                    nc.vector.tensor_tensor(out=t[:, n0 : n0 + HALF], in0=t[:, n0 : n0 + HALF], in1=bias[c][:, n0 : n0 + HALF], op=ALU.add)
            else:
                nc.gpsimd.tensor_tensor(out=t[:], in0=t[:], in1=bias[c], op=ALU.add)
            h0 = CHUNK_HEADS * c
            dst = out_0[0, h0 : h0 + CHUNK_HEADS, w].rearrange("h i d -> i h d")
            nc.sync.dma_start(out=dst, in_=t[:].rearrange("p (h d) -> p h d", d=HD))

        keep_bias(V_CHUNKS, spread_bias(V_CHUNKS), nc.vector.tensor_copy)
        transpose_x(0, 0)
        transpose_x(0, 1)
        keep_bias(K_CHUNKS, spread_bias(K_CHUNKS), nc.scalar.copy)
        keep_bias(Q_CHUNKS, spread_bias(Q_CHUNKS), nc.scalar.copy)
        quantize(0, 0)
        quantize(0, 1)
        key_value(0, V_CHUNKS[0], 0)
        transpose_x(0, 2)
        transpose_x(0, 3)
        key_value(0, V_CHUNKS[0], 1)
        quantize(0, 2)
        key_value(0, V_CHUNKS[1], 0)
        quantize(0, 3)
        regroup_for_q(nc.gpsimd.tensor_copy, kv_scales[0], q_scales[0])
        regroup_for_q(nc.scalar.copy, kv_codes[0], q_codes[0])
        key_value(0, V_CHUNKS[1], 1)
        for c in V_CHUNKS:
            for j in (2, 3):
                key_value(0, c, j)

        for w in range(WINDOWS):
            more = w + 1 < WINDOWS
            if more:
                split_words(w + 1, 0)
                split_words(w + 1, 2)
            for c in (V_CHUNKS if w > 0 else ()) + K_CHUNKS:
                for j in range(TILES):
                    key_value(w, c, j)
            if more:
                for j in range(TILES):
                    transpose_x(w + 1, j)
                for j in range(TILES):
                    quantize(w + 1, j)
                regroup_for_q(nc.gpsimd.tensor_copy, kv_scales[w + 1], q_scales[w + 1])
            for c in Q_CHUNKS:
                query(w, c, 0)
            for c in Q_CHUNKS:
                for m in range(1, TILES):
                    query(w, c, m)
                finish_query(w, c)
            if more:
                regroup_for_q(nc.scalar.copy, kv_codes[w + 1], q_codes[w + 1])
